import numpy as np
import ml_dtypes

BF16 = ml_dtypes.bfloat16


def bf(x):
    return np.asarray(x, np.float32).astype(BF16)


def f32(x):
    return np.asarray(x, np.float32)


def f64(x):
    return np.asarray(x).astype(np.float64)


def striped(idx):
    return np.tile(idx.reshape(-1, 16).T, (8, 1))


H, D, HALF, P, C, HID, S, N = 2, 64, 32, 128, 256, 256, 256, 128
ROPE_BASE = 10000.0


def rotary_table():
    inv = np.float32(1.0) / np.float32(ROPE_BASE) ** (np.arange(HALF, dtype=np.float32) / np.float32(HALF))
    t = inv[:, None] * np.arange(S, dtype=np.float32)[None, :]
    rows = np.arange(P)
    sgn = np.where(rows % D < HALF, -1.0, 1.0)[:, None]
    return np.concatenate([np.cos(t)[rows % HALF], sgn * np.sin(t)[rows % HALF]], axis=0)


def setup_inputs():
    return {"tab": f32(rotary_table()), "hidden": bf(np.random.standard_normal((HID, N))), "w": bf(np.random.standard_normal((HID, C)) / np.sqrt(HID)), "offs": striped(np.random.permutation(np.tile(np.arange(S), 2))[:N])}


def reference(tab, hidden, w, offs):
    idx = offs[:16].T.reshape(-1)
    y = f64(w).T @ f64(hidden)
    chan = np.arange(C)
    partner = (chan // D) * D + (chan + HALF) % D
    picked = f64(tab)[:, idx]
    return picked[:P][chan % P] * y + picked[P:][chan % P] * y[partner]

@@ -1,0 +1,75 @@
+import concourse.mybir as mybir
+
+BF16, F32, U16 = mybir.dt.bfloat16, mybir.dt.float32, mybir.dt.uint16
+MULT, ADD = mybir.AluOpType.mult, mybir.AluOpType.add
+
+P = 128
+HID = 256
+C = 256
+N = 128
+S = 256
+HALF = 32
+K_STEPS = HID // P
+BLOCKS = C // P
+QUADRANTS = P // HALF
+
+FLOPS = 2 * HID * C * N
+
+
+def tile_openbt5attention_kernel(tc, tab, hidden, w, offs, out):
+    nc = tc.nc
+    with (
+        tc.tile_pool(name="held", bufs=1) as held,
+        tc.psum_pool(name="psum", bufs=1) as psum,
+    ):
+        offsets = held.tile([P, N // 16], U16, name="offsets")
+        nc.sync.dma_start(offsets[:], offs)
+
+        w_sb = held.tile([P, K_STEPS, C], BF16, name="w_sb")
+        nc.sync.dma_start(w_sb[:], w.rearrange("(p k) c -> p k c", k=K_STEPS))
+        hidden_sb = held.tile([P, K_STEPS, N], BF16, name="hidden_sb")
+        nc.scalar.dma_start(hidden_sb[:], hidden.rearrange("(p k) j -> p k j", k=K_STEPS))
+
+        cos_tab = held.tile([P, S], F32, name="cos_tab")
+        nc.sync.dma_start(cos_tab[:], tab[0:P, :])
+        sin_tab = held.tile([P, S], F32, name="sin_tab")
+        nc.scalar.dma_start(sin_tab[:], tab[P : 2 * P, :])
+
+        y_psum = [psum.tile([P, N], F32, name=f"y_psum{b}") for b in range(BLOCKS)]
+        y = [held.tile([P, N], F32, name=f"y{b}") for b in range(BLOCKS)]
+        for b in range(BLOCKS):
+            for k in range(K_STEPS):
+                nc.tensor.matmul(
+                    y_psum[b][:],
+                    w_sb[:, k, b * P : (b + 1) * P],
+                    hidden_sb[:, k, :],
+                    start=(k == 0),
+                    stop=(k == K_STEPS - 1),
+                )
+            nc.scalar.copy(y[b][:], y_psum[b][:])
+
+        y_partner_psum = [psum.tile([P, N], F32, name=f"y_partner_psum{b}") for b in range(BLOCKS)]
+        y_partner = [held.tile([P, N], F32, name=f"y_partner{b}") for b in range(BLOCKS)]
+        for b in range(BLOCKS):
+            for q in range(QUADRANTS):
+                first = b * P + (q ^ 1) * HALF
+                for k in range(K_STEPS):
+                    nc.tensor.matmul(
+                        y_partner_psum[b][q * HALF : (q + 1) * HALF, :],
+                        w_sb[:, k, first : first + HALF],
+                        hidden_sb[:, k, :],
+                        start=(k == 0),
+                        stop=(k == K_STEPS - 1),
+                    )
+            nc.scalar.copy(y_partner[b][:], y_partner_psum[b][:])
+
+        cos_part = [held.tile([P, N], F32, name=f"cos_part{b}") for b in range(BLOCKS)]
+        sin_part = [held.tile([P, N], F32, name=f"sin_part{b}") for b in range(BLOCKS)]
+        rotated = [held.tile([P, N], F32, name=f"rotated{b}") for b in range(BLOCKS)]
+        for b in range(BLOCKS):
+            nc.vector.tensor_tensor(cos_part[b][:], cos_tab[:].indirect(offsets[:]), y[b][:], MULT)
+        for b in range(BLOCKS):
+            nc.vector.tensor_tensor(sin_part[b][:], sin_tab[:].indirect(offsets[:]), y_partner[b][:], MULT)
+            nc.vector.tensor_tensor(rotated[b][:], cos_part[b][:], sin_part[b][:], ADD)
+            store_queue = nc.sync if b == 0 else nc.scalar
+            store_queue.dma_start(out[b * P : (b + 1) * P, :], rotated[b][:])

@@ -11,7 +11,6 @@ S = 256
 HALF = 32
 K_STEPS = HID // P
 BLOCKS = C // P
-QUADRANTS = P // HALF
 
 FLOPS = 2 * HID * C * N
 
@@ -48,19 +47,24 @@ def tile_openbt5attention_kernel(tc, tab, hidden, w, offs, out):
                 )
             nc.scalar.copy(y[b][:], y_psum[b][:])
 
+        w_partner = held.tile([P, K_STEPS, C], BF16, name="w_partner")
+        by_halves = "p k (head half r) -> p k head half r"
+        w_halves = w_sb[:].rearrange(by_halves, half=2, r=HALF)
+        w_partner_halves = w_partner[:].rearrange(by_halves, half=2, r=HALF)
+        for half in range(2):
+            nc.vector.tensor_copy(w_partner_halves[:, :, :, half, :], w_halves[:, :, :, 1 - half, :])
+
         y_partner_psum = [psum.tile([P, N], F32, name=f"y_partner_psum{b}") for b in range(BLOCKS)]
         y_partner = [held.tile([P, N], F32, name=f"y_partner{b}") for b in range(BLOCKS)]
         for b in range(BLOCKS):
-            for q in range(QUADRANTS):
-                first = b * P + (q ^ 1) * HALF
-                for k in range(K_STEPS):
-                    nc.tensor.matmul(
-                        y_partner_psum[b][q * HALF : (q + 1) * HALF, :],
-                        w_sb[:, k, first : first + HALF],
-                        hidden_sb[:, k, :],
-                        start=(k == 0),
-                        stop=(k == K_STEPS - 1),
-                    )
+            for k in range(K_STEPS):
+                nc.tensor.matmul(
+                    y_partner_psum[b][:],
+                    w_partner[:, k, b * P : (b + 1) * P],
+                    hidden_sb[:, k, :],
+                    start=(k == 0),
+                    stop=(k == K_STEPS - 1),
+                )
             nc.scalar.copy(y_partner[b][:], y_partner_psum[b][:])
 
         cos_part = [held.tile([P, N], F32, name=f"cos_part{b}") for b in range(BLOCKS)]

@@ -21,18 +21,17 @@ def tile_openbt5attention_kernel(tc, tab, hidden, w, offs, out):
         tc.tile_pool(name="held", bufs=1) as held,
         tc.psum_pool(name="psum", bufs=1) as psum,
     ):
-        offsets = held.tile([P, N // 16], U16, name="offsets")
-        nc.sync.dma_start(offsets[:], offs)
-
         w_sb = held.tile([P, K_STEPS, C], BF16, name="w_sb")
         nc.sync.dma_start(w_sb[:], w.rearrange("(p k) c -> p k c", k=K_STEPS))
+        offsets = held.tile([P, N // 16], U16, name="offsets")
+        nc.sync.dma_start(offsets[:], offs)
         hidden_sb = held.tile([P, K_STEPS, N], BF16, name="hidden_sb")
         nc.scalar.dma_start(hidden_sb[:], hidden.rearrange("(p k) j -> p k j", k=K_STEPS))
 
         cos_tab = held.tile([P, S], F32, name="cos_tab")
-        nc.sync.dma_start(cos_tab[:], tab[0:P, :])
+        nc.scalar.dma_start(cos_tab[:], tab[0:P, :])
         sin_tab = held.tile([P, S], F32, name="sin_tab")
-        nc.scalar.dma_start(sin_tab[:], tab[P : 2 * P, :])
+        nc.sync.dma_start(sin_tab[:], tab[P : 2 * P, :])
 
         y_psum = [psum.tile([P, N], F32, name=f"y_psum{b}") for b in range(BLOCKS)]
         y = [held.tile([P, N], F32, name=f"y{b}") for b in range(BLOCKS)]
@@ -74,6 +73,7 @@ def tile_openbt5attention_kernel(tc, tab, hidden, w, offs, out):
             nc.vector.tensor_tensor(cos_part[b][:], cos_tab[:].indirect(offsets[:]), y[b][:], MULT)
         for b in range(BLOCKS):
             nc.vector.tensor_tensor(sin_part[b][:], sin_tab[:].indirect(offsets[:]), y_partner[b][:], MULT)
-            nc.vector.tensor_tensor(rotated[b][:], cos_part[b][:], sin_part[b][:], ADD)
+            add_engine = nc.gpsimd if b == 0 else nc.vector
+            add_engine.tensor_tensor(rotated[b][:], cos_part[b][:], sin_part[b][:], ADD)
             store_queue = nc.sync if b == 0 else nc.scalar
             store_queue.dma_start(out[b * P : (b + 1) * P, :], rotated[b][:])

@@ -33,19 +33,6 @@ def tile_openbt5attention_kernel(tc, tab, hidden, w, offs, out):
         sin_tab = held.tile([P, S], F32, name="sin_tab")
         nc.sync.dma_start(sin_tab[:], tab[P : 2 * P, :])
 
-        y_psum = [psum.tile([P, N], F32, name=f"y_psum{b}") for b in range(BLOCKS)]
-        y = [held.tile([P, N], F32, name=f"y{b}") for b in range(BLOCKS)]
-        for b in range(BLOCKS):
-            for k in range(K_STEPS):
-                nc.tensor.matmul(
-                    y_psum[b][:],
-                    w_sb[:, k, b * P : (b + 1) * P],
-                    hidden_sb[:, k, :],
-                    start=(k == 0),
-                    stop=(k == K_STEPS - 1),
-                )
-            nc.scalar.copy(y[b][:], y_psum[b][:])
-
         w_partner = held.tile([P, K_STEPS, C], BF16, name="w_partner")
         by_halves = "p k (head half r) -> p k head half r"
         w_halves = w_sb[:].rearrange(by_halves, half=2, r=HALF)
@@ -53,27 +40,31 @@ def tile_openbt5attention_kernel(tc, tab, hidden, w, offs, out):
         for half in range(2):
             nc.vector.tensor_copy(w_partner_halves[:, :, :, half, :], w_halves[:, :, :, 1 - half, :])
 
-        y_partner_psum = [psum.tile([P, N], F32, name=f"y_partner_psum{b}") for b in range(BLOCKS)]
-        y_partner = [held.tile([P, N], F32, name=f"y_partner{b}") for b in range(BLOCKS)]
         for b in range(BLOCKS):
-            for k in range(K_STEPS):
-                nc.tensor.matmul(
-                    y_partner_psum[b][:],
-                    w_partner[:, k, b * P : (b + 1) * P],
-                    hidden_sb[:, k, :],
-                    start=(k == 0),
-                    stop=(k == K_STEPS - 1),
-                )
-            nc.scalar.copy(y_partner[b][:], y_partner_psum[b][:])
+            projected = []
+            for name, weights in (("y", w_sb), ("y_partner", w_partner)):
+                product = psum.tile([P, N], F32, name=f"{name}_psum{b}")
+                for k in range(K_STEPS):
+                    nc.tensor.matmul(
+                        product[:],
+                        weights[:, k, b * P : (b + 1) * P],
+                        hidden_sb[:, k, :],
+                        start=(k == 0),
+                        stop=(k == K_STEPS - 1),
+                    )
+                in_sbuf = held.tile([P, N], F32, name=f"{name}{b}")
+                nc.scalar.copy(in_sbuf[:], product[:])
+                projected.append(in_sbuf)
+            y, y_partner = projected
 
-        cos_part = [held.tile([P, N], F32, name=f"cos_part{b}") for b in range(BLOCKS)]
-        sin_part = [held.tile([P, N], F32, name=f"sin_part{b}") for b in range(BLOCKS)]
-        rotated = [held.tile([P, N], F32, name=f"rotated{b}") for b in range(BLOCKS)]
-        for b in range(BLOCKS):
-            nc.vector.tensor_tensor(cos_part[b][:], cos_tab[:].indirect(offsets[:]), y[b][:], MULT)
-        for b in range(BLOCKS):
-            nc.vector.tensor_tensor(sin_part[b][:], sin_tab[:].indirect(offsets[:]), y_partner[b][:], MULT)
-            add_engine = nc.gpsimd if b == 0 else nc.vector
-            add_engine.tensor_tensor(rotated[b][:], cos_part[b][:], sin_part[b][:], ADD)
-            store_queue = nc.sync if b == 0 else nc.scalar
-            store_queue.dma_start(out[b * P : (b + 1) * P, :], rotated[b][:])
+            cos_part = held.tile([P, N], F32, name=f"cos_part{b}")
+            nc.vector.tensor_tensor(cos_part[:], cos_tab[:].indirect(offsets[:]), y[:], MULT)
+            sin_part = held.tile([P, N], F32, name=f"sin_part{b}")
+            nc.vector.tensor_tensor(sin_part[:], sin_tab[:].indirect(offsets[:]), y_partner[:], MULT)
+
+            last = b == BLOCKS - 1
+            rotated = held.tile([P, N], F32, name=f"rotated{b}")
+            add_engine = nc.vector if last else nc.gpsimd
+            add_engine.tensor_tensor(rotated[:], cos_part[:], sin_part[:], ADD)
+            store_queue = nc.sync if last else nc.scalar
+            store_queue.dma_start(out[b * P : (b + 1) * P, :], rotated[:])

@@ -23,15 +23,28 @@ def tile_openbt5attention_kernel(tc, tab, hidden, w, offs, out):
     ):
         w_sb = held.tile([P, K_STEPS, C], BF16, name="w_sb")
         nc.sync.dma_start(w_sb[:], w.rearrange("(p k) c -> p k c", k=K_STEPS))
+        hidden_sb = held.tile([P, K_STEPS, N], BF16, name="hidden_sb")
+        nc.sync.dma_start(hidden_sb[:], hidden.rearrange("(p k) j -> p k j", k=K_STEPS))
         offsets = held.tile([P, N // 16], U16, name="offsets")
         nc.sync.dma_start(offsets[:], offs)
-        hidden_sb = held.tile([P, K_STEPS, N], BF16, name="hidden_sb")
-        nc.scalar.dma_start(hidden_sb[:], hidden.rearrange("(p k) j -> p k j", k=K_STEPS))
 
         cos_tab = held.tile([P, S], F32, name="cos_tab")
-        nc.scalar.dma_start(cos_tab[:], tab[0:P, :])
+        nc.sync.dma_start(cos_tab[:], tab[0:P, :])
         sin_tab = held.tile([P, S], F32, name="sin_tab")
         nc.sync.dma_start(sin_tab[:], tab[P : 2 * P, :])
+
+        y_psum = [psum.tile([P, N], F32, name=f"y_psum{b}") for b in range(BLOCKS)]
+        y = [held.tile([P, N], F32, name=f"y{b}") for b in range(BLOCKS)]
+        for b in range(BLOCKS):
+            for k in range(K_STEPS):
+                nc.tensor.matmul(
+                    y_psum[b][:],
+                    w_sb[:, k, b * P : (b + 1) * P],
+                    hidden_sb[:, k, :],
+                    start=(k == 0),
+                    stop=(k == K_STEPS - 1),
+                )
+            nc.scalar.copy(y[b][:], y_psum[b][:])
 
         w_partner = held.tile([P, K_STEPS, C], BF16, name="w_partner")
         by_halves = "p k (head half r) -> p k head half r"
@@ -40,31 +53,26 @@ def tile_openbt5attention_kernel(tc, tab, hidden, w, offs, out):
         for half in range(2):
             nc.vector.tensor_copy(w_partner_halves[:, :, :, half, :], w_halves[:, :, :, 1 - half, :])
 
+        y_partner_psum = [psum.tile([P, N], F32, name=f"y_partner_psum{b}") for b in range(BLOCKS)]
+        y_partner = [held.tile([P, N], F32, name=f"y_partner{b}") for b in range(BLOCKS)]
         for b in range(BLOCKS):
-            projected = []
-            for name, weights in (("y", w_sb), ("y_partner", w_partner)):
-                product = psum.tile([P, N], F32, name=f"{name}_psum{b}")
-                for k in range(K_STEPS):
-                    nc.tensor.matmul(
-                        product[:],
-                        weights[:, k, b * P : (b + 1) * P],
-                        hidden_sb[:, k, :],
-                        start=(k == 0),
-                        stop=(k == K_STEPS - 1),
-                    )
-                in_sbuf = held.tile([P, N], F32, name=f"{name}{b}")
-                nc.scalar.copy(in_sbuf[:], product[:])
-                projected.append(in_sbuf)
-            y, y_partner = projected
+            for k in range(K_STEPS):
+                nc.tensor.matmul(
+                    y_partner_psum[b][:],
+                    w_partner[:, k, b * P : (b + 1) * P],
+                    hidden_sb[:, k, :],
+                    start=(k == 0),
+                    stop=(k == K_STEPS - 1),
+                )
+            nc.scalar.copy(y_partner[b][:], y_partner_psum[b][:])
 
-            cos_part = held.tile([P, N], F32, name=f"cos_part{b}")
-            nc.vector.tensor_tensor(cos_part[:], cos_tab[:].indirect(offsets[:]), y[:], MULT)
-            sin_part = held.tile([P, N], F32, name=f"sin_part{b}")
-            nc.vector.tensor_tensor(sin_part[:], sin_tab[:].indirect(offsets[:]), y_partner[:], MULT)
-
-            last = b == BLOCKS - 1
-            rotated = held.tile([P, N], F32, name=f"rotated{b}")
-            add_engine = nc.vector if last else nc.gpsimd
-            add_engine.tensor_tensor(rotated[:], cos_part[:], sin_part[:], ADD)
-            store_queue = nc.sync if last else nc.scalar
-            store_queue.dma_start(out[b * P : (b + 1) * P, :], rotated[:])
+        cos_part = [held.tile([P, N], F32, name=f"cos_part{b}") for b in range(BLOCKS)]
+        sin_part = [held.tile([P, N], F32, name=f"sin_part{b}") for b in range(BLOCKS)]
+        rotated = [held.tile([P, N], F32, name=f"rotated{b}") for b in range(BLOCKS)]
+        for b in range(BLOCKS):
+            nc.vector.tensor_tensor(cos_part[b][:], cos_tab[:].indirect(offsets[:]), y[b][:], MULT)
+        for b in range(BLOCKS):
+            nc.vector.tensor_tensor(sin_part[b][:], sin_tab[:].indirect(offsets[:]), y_partner[b][:], MULT)
+            nc.vector.tensor_tensor(rotated[b][:], cos_part[b][:], sin_part[b][:], ADD)
+            store_queue = nc.sync if b == 0 else nc.scalar
+            store_queue.dma_start(out[b * P : (b + 1) * P, :], rotated[b][:])

@@ -15,6 +15,19 @@ BLOCKS = C // P
 FLOPS = 2 * HID * C * N
 
 
+def project(nc, psum, weights, hidden_sb, b, name):
+    product = psum.tile([P, N], F32, name=name)
+    for k in range(K_STEPS):
+        nc.tensor.matmul(
+            product[:],
+            weights[:, k, b * P : (b + 1) * P],
+            hidden_sb[:, k, :],
+            start=(k == 0),
+            stop=(k == K_STEPS - 1),
+        )
+    return product
+
+
 def tile_openbt5attention_kernel(tc, tab, hidden, w, offs, out):
     nc = tc.nc
     with (
@@ -33,19 +46,6 @@ def tile_openbt5attention_kernel(tc, tab, hidden, w, offs, out):
         sin_tab = held.tile([P, S], F32, name="sin_tab")
         nc.sync.dma_start(sin_tab[:], tab[P : 2 * P, :])
 
-        y_psum = [psum.tile([P, N], F32, name=f"y_psum{b}") for b in range(BLOCKS)]
-        y = [held.tile([P, N], F32, name=f"y{b}") for b in range(BLOCKS)]
-        for b in range(BLOCKS):
-            for k in range(K_STEPS):
-                nc.tensor.matmul(
-                    y_psum[b][:],
-                    w_sb[:, k, b * P : (b + 1) * P],
-                    hidden_sb[:, k, :],
-                    start=(k == 0),
-                    stop=(k == K_STEPS - 1),
-                )
-            nc.scalar.copy(y[b][:], y_psum[b][:])
-
         w_partner = held.tile([P, K_STEPS, C], BF16, name="w_partner")
         by_halves = "p k (head half r) -> p k head half r"
         w_halves = w_sb[:].rearrange(by_halves, half=2, r=HALF)
@@ -53,18 +53,13 @@ def tile_openbt5attention_kernel(tc, tab, hidden, w, offs, out):
         for half in range(2):
             nc.vector.tensor_copy(w_partner_halves[:, :, :, half, :], w_halves[:, :, :, 1 - half, :])
 
-        y_partner_psum = [psum.tile([P, N], F32, name=f"y_partner_psum{b}") for b in range(BLOCKS)]
+        y = [held.tile([P, N], F32, name=f"y{b}") for b in range(BLOCKS)]
         y_partner = [held.tile([P, N], F32, name=f"y_partner{b}") for b in range(BLOCKS)]
+        nc.vector.tensor_copy(y[0][:], project(nc, psum, w_sb, hidden_sb, 0, "y_psum0")[:])
+        for b in range(1, BLOCKS):
+            nc.scalar.copy(y[b][:], project(nc, psum, w_sb, hidden_sb, b, f"y_psum{b}")[:])
         for b in range(BLOCKS):
-            for k in range(K_STEPS):
-                nc.tensor.matmul(
-                    y_partner_psum[b][:],
-                    w_partner[:, k, b * P : (b + 1) * P],
-                    hidden_sb[:, k, :],
-                    start=(k == 0),
-                    stop=(k == K_STEPS - 1),
-                )
-            nc.scalar.copy(y_partner[b][:], y_partner_psum[b][:])
+            nc.scalar.copy(y_partner[b][:], project(nc, psum, w_partner, hidden_sb, b, f"y_partner_psum{b}")[:])
 
         cos_part = [held.tile([P, N], F32, name=f"cos_part{b}") for b in range(BLOCKS)]
         sin_part = [held.tile([P, N], F32, name=f"sin_part{b}") for b in range(BLOCKS)]
@@ -74,5 +69,4 @@ def tile_openbt5attention_kernel(tc, tab, hidden, w, offs, out):
         for b in range(BLOCKS):
             nc.vector.tensor_tensor(sin_part[b][:], sin_tab[:].indirect(offsets[:]), y_partner[b][:], MULT)
             nc.vector.tensor_tensor(rotated[b][:], cos_part[b][:], sin_part[b][:], ADD)
-            store_queue = nc.sync if b == 0 else nc.scalar
-            store_queue.dma_start(out[b * P : (b + 1) * P, :], rotated[b][:])
+            nc.sync.dma_start(out[b * P : (b + 1) * P, :], rotated[b][:])

@@ -37,7 +37,7 @@ def tile_openbt5attention_kernel(tc, tab, hidden, w, offs, out):
         w_sb = held.tile([P, K_STEPS, C], BF16, name="w_sb")
         nc.sync.dma_start(w_sb[:], w.rearrange("(p k) c -> p k c", k=K_STEPS))
         hidden_sb = held.tile([P, K_STEPS, N], BF16, name="hidden_sb")
-        nc.sync.dma_start(hidden_sb[:], hidden.rearrange("(p k) j -> p k j", k=K_STEPS))
+        nc.scalar.dma_start(hidden_sb[:], hidden.rearrange("(p k) j -> p k j", k=K_STEPS))
         offsets = held.tile([P, N // 16], U16, name="offsets")
         nc.sync.dma_start(offsets[:], offs)
 

@@ -56,17 +56,15 @@ def tile_openbt5attention_kernel(tc, tab, hidden, w, offs, out):
         y = [held.tile([P, N], F32, name=f"y{b}") for b in range(BLOCKS)]
         y_partner = [held.tile([P, N], F32, name=f"y_partner{b}") for b in range(BLOCKS)]
         nc.vector.tensor_copy(y[0][:], project(nc, psum, w_sb, hidden_sb, 0, "y_psum0")[:])
-        for b in range(1, BLOCKS):
-            nc.scalar.copy(y[b][:], project(nc, psum, w_sb, hidden_sb, b, f"y_psum{b}")[:])
-        for b in range(BLOCKS):
-            nc.scalar.copy(y_partner[b][:], project(nc, psum, w_partner, hidden_sb, b, f"y_partner_psum{b}")[:])
+        nc.scalar.copy(y_partner[0][:], project(nc, psum, w_partner, hidden_sb, 0, "y_partner_psum0")[:])
+        nc.scalar.copy(y[1][:], project(nc, psum, w_sb, hidden_sb, 1, "y_psum1")[:])
+        nc.scalar.copy(y_partner[1][:], project(nc, psum, w_partner, hidden_sb, 1, "y_partner_psum1")[:])
 
         cos_part = [held.tile([P, N], F32, name=f"cos_part{b}") for b in range(BLOCKS)]
         sin_part = [held.tile([P, N], F32, name=f"sin_part{b}") for b in range(BLOCKS)]
         rotated = [held.tile([P, N], F32, name=f"rotated{b}") for b in range(BLOCKS)]
         for b in range(BLOCKS):
             nc.vector.tensor_tensor(cos_part[b][:], cos_tab[:].indirect(offsets[:]), y[b][:], MULT)
-        for b in range(BLOCKS):
             nc.vector.tensor_tensor(sin_part[b][:], sin_tab[:].indirect(offsets[:]), y_partner[b][:], MULT)
             nc.vector.tensor_tensor(rotated[b][:], cos_part[b][:], sin_part[b][:], ADD)
             nc.sync.dma_start(out[b * P : (b + 1) * P, :], rotated[b][:])

@@ -35,9 +35,9 @@ def tile_openbt5attention_kernel(tc, tab, hidden, w, offs, out):
         tc.psum_pool(name="psum", bufs=1) as psum,
     ):
         w_sb = held.tile([P, K_STEPS, C], BF16, name="w_sb")
-        nc.sync.dma_start(w_sb[:], w.rearrange("(p k) c -> p k c", k=K_STEPS))
+        nc.scalar.dma_start(w_sb[:], w.rearrange("(p k) c -> p k c", k=K_STEPS))
         hidden_sb = held.tile([P, K_STEPS, N], BF16, name="hidden_sb")
-        nc.scalar.dma_start(hidden_sb[:], hidden.rearrange("(p k) j -> p k j", k=K_STEPS))
+        nc.sync.dma_start(hidden_sb[:], hidden.rearrange("(p k) j -> p k j", k=K_STEPS))
         offsets = held.tile([P, N // 16], U16, name="offsets")
         nc.sync.dma_start(offsets[:], offs)
 

@@ -50,8 +50,8 @@ def tile_openbt5attention_kernel(tc, tab, hidden, w, offs, out):
         by_halves = "p k (head half r) -> p k head half r"
         w_halves = w_sb[:].rearrange(by_halves, half=2, r=HALF)
         w_partner_halves = w_partner[:].rearrange(by_halves, half=2, r=HALF)
-        for half in range(2):
-            nc.vector.tensor_copy(w_partner_halves[:, :, :, half, :], w_halves[:, :, :, 1 - half, :])
+        nc.vector.tensor_copy(w_partner_halves[:, :, :, 0, :], w_halves[:, :, :, 1, :])
+        nc.scalar.copy(w_partner_halves[:, :, :, 1, :], w_halves[:, :, :, 0, :])
 
         y = [held.tile([P, N], F32, name=f"y{b}") for b in range(BLOCKS)]
         y_partner = [held.tile([P, N], F32, name=f"y_partner{b}") for b in range(BLOCKS)]

import concourse.mybir as mybir

BF16, F32, U16 = mybir.dt.bfloat16, mybir.dt.float32, mybir.dt.uint16
MULT, ADD = mybir.AluOpType.mult, mybir.AluOpType.add

P = 128
HID = 256
C = 256
N = 128
S = 256
HALF = 32
K_STEPS = HID // P
BLOCKS = C // P

FLOPS = 2 * HID * C * N


def project(nc, psum, weights, hidden_sb, b, name):
    product = psum.tile([P, N], F32, name=name)
    for k in range(K_STEPS):
        nc.tensor.matmul(
            product[:],
            weights[:, k, b * P : (b + 1) * P],
            hidden_sb[:, k, :],
            start=(k == 0),
            stop=(k == K_STEPS - 1),
        )
    return product


def tile_openbt5attention_kernel(tc, tab, hidden, w, offs, out):
    nc = tc.nc
    with (
        tc.tile_pool(name="held", bufs=1) as held,
        tc.psum_pool(name="psum", bufs=1) as psum,
    ):
        w_sb = held.tile([P, K_STEPS, C], BF16, name="w_sb")
        nc.scalar.dma_start(w_sb[:], w.rearrange("(p k) c -> p k c", k=K_STEPS))
        hidden_sb = held.tile([P, K_STEPS, N], BF16, name="hidden_sb")
        nc.sync.dma_start(hidden_sb[:], hidden.rearrange("(p k) j -> p k j", k=K_STEPS))
        offsets = held.tile([P, N // 16], U16, name="offsets")
        nc.sync.dma_start(offsets[:], offs)

        cos_tab = held.tile([P, S], F32, name="cos_tab")
        nc.sync.dma_start(cos_tab[:], tab[0:P, :])
        sin_tab = held.tile([P, S], F32, name="sin_tab")
        nc.sync.dma_start(sin_tab[:], tab[P : 2 * P, :])

        w_partner = held.tile([P, K_STEPS, C], BF16, name="w_partner")
        by_halves = "p k (head half r) -> p k head half r"
        w_halves = w_sb[:].rearrange(by_halves, half=2, r=HALF)
        w_partner_halves = w_partner[:].rearrange(by_halves, half=2, r=HALF)
        nc.vector.tensor_copy(w_partner_halves[:, :, :, 0, :], w_halves[:, :, :, 1, :])
        nc.scalar.copy(w_partner_halves[:, :, :, 1, :], w_halves[:, :, :, 0, :])

        y = [held.tile([P, N], F32, name=f"y{b}") for b in range(BLOCKS)]
        y_partner = [held.tile([P, N], F32, name=f"y_partner{b}") for b in range(BLOCKS)]
        nc.vector.tensor_copy(y[0][:], project(nc, psum, w_sb, hidden_sb, 0, "y_psum0")[:])
        nc.scalar.copy(y_partner[0][:], project(nc, psum, w_partner, hidden_sb, 0, "y_partner_psum0")[:])
        nc.scalar.copy(y[1][:], project(nc, psum, w_sb, hidden_sb, 1, "y_psum1")[:])
        nc.scalar.copy(y_partner[1][:], project(nc, psum, w_partner, hidden_sb, 1, "y_partner_psum1")[:])

        cos_part = [held.tile([P, N], F32, name=f"cos_part{b}") for b in range(BLOCKS)]
        sin_part = [held.tile([P, N], F32, name=f"sin_part{b}") for b in range(BLOCKS)]
        rotated = [held.tile([P, N], F32, name=f"rotated{b}") for b in range(BLOCKS)]
        for b in range(BLOCKS):
            nc.vector.tensor_tensor(cos_part[b][:], cos_tab[:].indirect(offsets[:]), y[b][:], MULT)
            nc.vector.tensor_tensor(sin_part[b][:], sin_tab[:].indirect(offsets[:]), y_partner[b][:], MULT)
            nc.vector.tensor_tensor(rotated[b][:], cos_part[b][:], sin_part[b][:], ADD)
            nc.sync.dma_start(out[b * P : (b + 1) * P, :], rotated[b][:])
